import numpy as np
import ml_dtypes

BF16 = ml_dtypes.bfloat16


def bf(x):
    return np.asarray(x, np.float32).astype(BF16)


def f32(x):
    return np.asarray(x, np.float32)


def f64(x):
    return np.asarray(x).astype(np.float64)


def striped(idx):
    return np.tile(idx.reshape(-1, 16).T, (8, 1))


C, H, S, N = 256, 128, 1024, 512
ERF_LIM, ERF_TERMS = 6.0, 150
LORA_SCALE, BIAS_SCALE = 2.0, 0.2


def erf(a):
    c = np.clip(a, -ERF_LIM, ERF_LIM)
    term = c.copy()
    tot = c.copy()
    for n in range(1, ERF_TERMS):
        term = term * (2.0 * c * c) / (2.0 * n + 1.0)
        tot = tot + term
    return np.where(np.abs(a) > ERF_LIM, np.sign(a), 2.0 / np.sqrt(np.pi) * np.exp(-c * c) * tot)


def gelu_erf(v):
    return 0.5 * v * (1.0 + erf(v / np.sqrt(2.0)))


def setup_inputs():
    return {"h": f32(np.random.standard_normal((H, N))), "lora": f32(LORA_SCALE * np.random.standard_normal((C, S))), "lorab": f32(LORA_SCALE * np.random.standard_normal((C, 1))), "w": bf(np.random.standard_normal((H, H)) / np.sqrt(H)), "b": f32(BIAS_SCALE * np.random.standard_normal((H, 1))), "offs": striped(np.random.permutation(S)[:N])}


def reference(h, lora, lorab, w, b, offs):
    idx = offs[:16].T.reshape(-1)
    x = gelu_erf(f64(h))
    tab = f64(lora) + f64(lorab)
    p = tab[H:, idx] * x
    m = p.sum(axis=0, keepdims=True) / H
    z = tab[:H, idx] * m
    return gelu_erf(f64(w).T @ x + f64(b) + z)

@@ -1,0 +1,70 @@
+import concourse.mybir as mybir
+
+F32, BF16, U16 = mybir.dt.float32, mybir.dt.bfloat16, mybir.dt.uint16
+ACT = mybir.ActivationFunctionType
+ALU = mybir.AluOpType
+
+P = 128
+S = 1024
+N = 512
+
+FLOPS = 2 * P * P * N + 2 * P * N + 2 * P * N
+BYTES = 4 * P * N + 4 * 2 * P * N + 4 * 2 * P + 2 * P * P + 4 * P + 2 * P * (N // 16) + 4 * P * N
+
+
+def tile_multisubjectniirfpeft_kernel(tc, h, lora, lorab, w, b, offs, out):
+    nc = tc.nc
+    with (
+        tc.tile_pool(name="held", bufs=1) as held,
+        tc.psum_pool(name="psum", bufs=1) as psum,
+    ):
+        offsets = held.tile([P, N // 16], U16, name="offsets")
+        nc.sync.dma_start(offsets[:], offs)
+        h_sb = held.tile([P, N], F32, name="h_sb")
+        nc.sync.dma_start(h_sb[:], h)
+        lora_in = held.tile([P, S], F32, name="lora_in")
+        nc.sync.dma_start(lora_in[:], lora[P : 2 * P, :])
+        lora_out = held.tile([P, S], F32, name="lora_out")
+        nc.sync.dma_start(lora_out[:], lora[0:P, :])
+        bias_in = held.tile([P, 1], F32, name="bias_in")
+        nc.scalar.dma_start(bias_in[:], lorab[P : 2 * P, :])
+        bias_out = held.tile([P, 1], F32, name="bias_out")
+        nc.scalar.dma_start(bias_out[:], lorab[0:P, :])
+        w_sb = held.tile([P, P], BF16, name="w_sb")
+        nc.scalar.dma_start(w_sb[:], w)
+        b_sb = held.tile([P, 1], F32, name="b_sb")
+        nc.scalar.dma_start(b_sb[:], b)
+
+        mean_w = held.tile([P, P], BF16, name="mean_w")
+        nc.gpsimd.memset(mean_w[:], 1.0 / P)
+
+        x = held.tile([P, N], F32, name="x")
+        nc.scalar.activation(x[:], h_sb[:], ACT.Gelu)
+        x_bf = held.tile([P, N], BF16, name="x_bf")
+        nc.gpsimd.tensor_copy(x_bf[:], x[:])
+
+        tab_in = held.tile([P, S], F32, name="tab_in")
+        nc.vector.tensor_scalar_add(tab_in[:], lora_in[:], bias_in[:, 0:1])
+        tab_out = held.tile([P, S], F32, name="tab_out")
+        nc.scalar.activation(tab_out[:], lora_out[:], ACT.Identity, bias=bias_out[:, 0:1])
+
+        p = held.tile([P, N], F32, name="p")
+        nc.vector.tensor_tensor(p[:], tab_in[:].indirect(offsets[:]), x[:], ALU.mult)
+        p_bf = held.tile([P, N], BF16, name="p_bf")
+        nc.scalar.copy(p_bf[:], p[:])
+
+        m_ps = psum.tile([P, N], F32, name="m_ps")
+        nc.tensor.matmul(m_ps[:], mean_w[:], p_bf[:], start=True, stop=True)
+        m = held.tile([P, N], F32, name="m")
+        nc.scalar.copy(m[:], m_ps[:])
+
+        z = held.tile([P, N], F32, name="z")
+        nc.vector.tensor_tensor(z[:], tab_out[:].indirect(offsets[:]), m[:], ALU.mult)
+
+        y_ps = psum.tile([P, N], F32, name="y_ps")
+        nc.tensor.matmul(y_ps[:], w_sb[:], x_bf[:], start=True, stop=True)
+        y = held.tile([P, N], F32, name="y")
+        nc.vector.tensor_tensor(y[:], y_ps[:], z[:], ALU.add)
+        out_sb = held.tile([P, N], F32, name="out_sb")
+        nc.scalar.activation(out_sb[:], y[:], ACT.Gelu, bias=b_sb[:, 0:1])
+        nc.sync.dma_start(out, out_sb[:])

@@ -11,6 +11,10 @@ N = 512
 FLOPS = 2 * P * P * N + 2 * P * N + 2 * P * N
 BYTES = 4 * P * N + 4 * 2 * P * N + 4 * 2 * P + 2 * P * P + 4 * P + 2 * P * (N // 16) + 4 * P * N
 
+PIECE = 128
+PIECES = N // PIECE
+HALF = S // 2
+
 
 def tile_multisubjectniirfpeft_kernel(tc, h, lora, lorab, w, b, offs, out):
     nc = tc.nc
@@ -23,48 +27,64 @@ def tile_multisubjectniirfpeft_kernel(tc, h, lora, lorab, w, b, offs, out):
         h_sb = held.tile([P, N], F32, name="h_sb")
         nc.sync.dma_start(h_sb[:], h)
         lora_in = held.tile([P, S], F32, name="lora_in")
-        nc.sync.dma_start(lora_in[:], lora[P : 2 * P, :])
         lora_out = held.tile([P, S], F32, name="lora_out")
-        nc.sync.dma_start(lora_out[:], lora[0:P, :])
+        for half in range(2):
+            part = slice(half * HALF, (half + 1) * HALF)
+            nc.sync.dma_start(lora_in[:, part], lora[P : 2 * P, part])
+        for half in range(2):
+            part = slice(half * HALF, (half + 1) * HALF)
+            nc.sync.dma_start(lora_out[:, part], lora[0:P, part])
         bias_in = held.tile([P, 1], F32, name="bias_in")
         nc.scalar.dma_start(bias_in[:], lorab[P : 2 * P, :])
-        bias_out = held.tile([P, 1], F32, name="bias_out")
-        nc.scalar.dma_start(bias_out[:], lorab[0:P, :])
         w_sb = held.tile([P, P], BF16, name="w_sb")
         nc.scalar.dma_start(w_sb[:], w)
+        bias_out = held.tile([P, 1], F32, name="bias_out")
+        nc.gpsimd.dma_start(bias_out[:], lorab[0:P, :])
         b_sb = held.tile([P, 1], F32, name="b_sb")
-        nc.scalar.dma_start(b_sb[:], b)
+        nc.gpsimd.dma_start(b_sb[:], b)
 
         mean_w = held.tile([P, P], BF16, name="mean_w")
-        nc.gpsimd.memset(mean_w[:], 1.0 / P)
+        nc.vector.memset(mean_w[:], 1.0 / P)
 
         x = held.tile([P, N], F32, name="x")
         nc.scalar.activation(x[:], h_sb[:], ACT.Gelu)
         x_bf = held.tile([P, N], BF16, name="x_bf")
-        nc.gpsimd.tensor_copy(x_bf[:], x[:])
-
-        tab_in = held.tile([P, S], F32, name="tab_in")
-        nc.vector.tensor_scalar_add(tab_in[:], lora_in[:], bias_in[:, 0:1])
-        tab_out = held.tile([P, S], F32, name="tab_out")
-        nc.scalar.activation(tab_out[:], lora_out[:], ACT.Identity, bias=bias_out[:, 0:1])
-
-        p = held.tile([P, N], F32, name="p")
-        nc.vector.tensor_tensor(p[:], tab_in[:].indirect(offsets[:]), x[:], ALU.mult)
-        p_bf = held.tile([P, N], BF16, name="p_bf")
-        nc.scalar.copy(p_bf[:], p[:])
-
-        m_ps = psum.tile([P, N], F32, name="m_ps")
-        nc.tensor.matmul(m_ps[:], mean_w[:], p_bf[:], start=True, stop=True)
-        m = held.tile([P, N], F32, name="m")
-        nc.scalar.copy(m[:], m_ps[:])
-
-        z = held.tile([P, N], F32, name="z")
-        nc.vector.tensor_tensor(z[:], tab_out[:].indirect(offsets[:]), m[:], ALU.mult)
-
+        nc.scalar.copy(x_bf[:], x[:])
         y_ps = psum.tile([P, N], F32, name="y_ps")
         nc.tensor.matmul(y_ps[:], w_sb[:], x_bf[:], start=True, stop=True)
+
+        tab_in = held.tile([P, S], F32, name="tab_in")
+        tab_out = held.tile([P, S], F32, name="tab_out")
+        for half in range(2):
+            part = slice(half * HALF, (half + 1) * HALF)
+            nc.vector.tensor_scalar_add(tab_in[:, part], lora_in[:, part], bias_in[:, 0:1])
+
+        p = held.tile([P, N], F32, name="p")
+        p_bf = held.tile([P, N], BF16, name="p_bf")
+        m_ps = [psum.tile([P, PIECE], F32, name=f"m_ps{i}") for i in range(PIECES)]
+        m = held.tile([P, N], F32, name="m")
+        for i in range(PIECES + 1):
+            if i < PIECES:
+                cols = slice(i * PIECE, (i + 1) * PIECE)
+                listed = offsets[:, i * (PIECE // 16) : (i + 1) * (PIECE // 16)]
+                nc.vector.tensor_tensor(p[:, cols], tab_in[:].indirect(listed), x[:, cols], ALU.mult)
+                nc.scalar.copy(p_bf[:, cols], p[:, cols])
+                nc.tensor.matmul(m_ps[i][:], mean_w[:], p_bf[:, cols], start=True, stop=True)
+            if i == 0:
+                nc.scalar.activation(
+                    tab_out[:, 0:HALF], lora_out[:, 0:HALF], ACT.Identity, bias=bias_out[:, 0:1]
+                )
+            if i > 0:
+                nc.scalar.copy(m[:, (i - 1) * PIECE : i * PIECE], m_ps[i - 1][:])
+        nc.vector.tensor_scalar_add(tab_out[:, HALF:S], lora_out[:, HALF:S], bias_out[:, 0:1])
+
+        z = held.tile([P, N], F32, name="z")
         y = held.tile([P, N], F32, name="y")
-        nc.vector.tensor_tensor(y[:], y_ps[:], z[:], ALU.add)
         out_sb = held.tile([P, N], F32, name="out_sb")
-        nc.scalar.activation(out_sb[:], y[:], ACT.Gelu, bias=b_sb[:, 0:1])
-        nc.sync.dma_start(out, out_sb[:])
+        for i in range(PIECES):
+            cols = slice(i * PIECE, (i + 1) * PIECE)
+            listed = offsets[:, i * (PIECE // 16) : (i + 1) * (PIECE // 16)]
+            nc.vector.tensor_tensor(z[:, cols], tab_out[:].indirect(listed), m[:, cols], ALU.mult)
+            nc.vector.tensor_tensor(y[:, cols], y_ps[:, cols], z[:, cols], ALU.add)
+            nc.scalar.activation(out_sb[:, cols], y[:, cols], ACT.Gelu, bias=b_sb[:, 0:1])
+            nc.sync.dma_start(out[:, cols], out_sb[:, cols])

@@ -11,7 +11,7 @@ N = 512
 FLOPS = 2 * P * P * N + 2 * P * N + 2 * P * N
 BYTES = 4 * P * N + 4 * 2 * P * N + 4 * 2 * P + 2 * P * P + 4 * P + 2 * P * (N // 16) + 4 * P * N
 
-PIECE = 128
+PIECE = 256
 PIECES = N // PIECE
 HALF = S // 2
 

@@ -11,7 +11,7 @@ N = 512
 FLOPS = 2 * P * P * N + 2 * P * N + 2 * P * N
 BYTES = 4 * P * N + 4 * 2 * P * N + 4 * 2 * P + 2 * P * P + 4 * P + 2 * P * (N // 16) + 4 * P * N
 
-PIECE = 256
+PIECE = 128
 PIECES = N // PIECE
 HALF = S // 2
 
@@ -27,21 +27,19 @@ def tile_multisubjectniirfpeft_kernel(tc, h, lora, lorab, w, b, offs, out):
         h_sb = held.tile([P, N], F32, name="h_sb")
         nc.sync.dma_start(h_sb[:], h)
         lora_in = held.tile([P, S], F32, name="lora_in")
-        lora_out = held.tile([P, S], F32, name="lora_out")
         for half in range(2):
             part = slice(half * HALF, (half + 1) * HALF)
             nc.sync.dma_start(lora_in[:, part], lora[P : 2 * P, part])
-        for half in range(2):
-            part = slice(half * HALF, (half + 1) * HALF)
-            nc.sync.dma_start(lora_out[:, part], lora[0:P, part])
+        lora_out = held.tile([P, S], F32, name="lora_out")
+        nc.sync.dma_start(lora_out[:], lora[0:P, :])
         bias_in = held.tile([P, 1], F32, name="bias_in")
         nc.scalar.dma_start(bias_in[:], lorab[P : 2 * P, :])
         w_sb = held.tile([P, P], BF16, name="w_sb")
         nc.scalar.dma_start(w_sb[:], w)
         bias_out = held.tile([P, 1], F32, name="bias_out")
-        nc.gpsimd.dma_start(bias_out[:], lorab[0:P, :])
+        nc.scalar.dma_start(bias_out[:], lorab[0:P, :])
         b_sb = held.tile([P, 1], F32, name="b_sb")
-        nc.gpsimd.dma_start(b_sb[:], b)
+        nc.scalar.dma_start(b_sb[:], b)
 
         mean_w = held.tile([P, P], BF16, name="mean_w")
         nc.vector.memset(mean_w[:], 1.0 / P)
@@ -49,12 +47,11 @@ def tile_multisubjectniirfpeft_kernel(tc, h, lora, lorab, w, b, offs, out):
         x = held.tile([P, N], F32, name="x")
         nc.scalar.activation(x[:], h_sb[:], ACT.Gelu)
         x_bf = held.tile([P, N], BF16, name="x_bf")
-        nc.scalar.copy(x_bf[:], x[:])
+        nc.scalar.activation(x_bf[:], h_sb[:], ACT.Gelu)
         y_ps = psum.tile([P, N], F32, name="y_ps")
         nc.tensor.matmul(y_ps[:], w_sb[:], x_bf[:], start=True, stop=True)
 
         tab_in = held.tile([P, S], F32, name="tab_in")
-        tab_out = held.tile([P, S], F32, name="tab_out")
         for half in range(2):
             part = slice(half * HALF, (half + 1) * HALF)
             nc.vector.tensor_scalar_add(tab_in[:, part], lora_in[:, part], bias_in[:, 0:1])
@@ -63,20 +60,16 @@ def tile_multisubjectniirfpeft_kernel(tc, h, lora, lorab, w, b, offs, out):
         p_bf = held.tile([P, N], BF16, name="p_bf")
         m_ps = [psum.tile([P, PIECE], F32, name=f"m_ps{i}") for i in range(PIECES)]
         m = held.tile([P, N], F32, name="m")
-        for i in range(PIECES + 1):
-            if i < PIECES:
-                cols = slice(i * PIECE, (i + 1) * PIECE)
-                listed = offsets[:, i * (PIECE // 16) : (i + 1) * (PIECE // 16)]
-                nc.vector.tensor_tensor(p[:, cols], tab_in[:].indirect(listed), x[:, cols], ALU.mult)
-                nc.scalar.copy(p_bf[:, cols], p[:, cols])
-                nc.tensor.matmul(m_ps[i][:], mean_w[:], p_bf[:, cols], start=True, stop=True)
-            if i == 0:
-                nc.scalar.activation(
-                    tab_out[:, 0:HALF], lora_out[:, 0:HALF], ACT.Identity, bias=bias_out[:, 0:1]
-                )
-            if i > 0:
-                nc.scalar.copy(m[:, (i - 1) * PIECE : i * PIECE], m_ps[i - 1][:])
-        nc.vector.tensor_scalar_add(tab_out[:, HALF:S], lora_out[:, HALF:S], bias_out[:, 0:1])
+        for i in range(PIECES):
+            cols = slice(i * PIECE, (i + 1) * PIECE)
+            listed = offsets[:, i * (PIECE // 16) : (i + 1) * (PIECE // 16)]
+            nc.vector.tensor_tensor(p[:, cols], tab_in[:].indirect(listed), x[:, cols], ALU.mult)
+            nc.scalar.copy(p_bf[:, cols], p[:, cols])
+            nc.tensor.matmul(m_ps[i][:], mean_w[:], p_bf[:, cols], start=True, stop=True)
+            nc.scalar.copy(m[:, cols], m_ps[i][:])
+
+        tab_out = held.tile([P, S], F32, name="tab_out")
+        nc.vector.tensor_scalar_add(tab_out[:], lora_out[:], bias_out[:, 0:1])
 
         z = held.tile([P, N], F32, name="z")
         y = held.tile([P, N], F32, name="y")

@@ -27,11 +27,13 @@ def tile_multisubjectniirfpeft_kernel(tc, h, lora, lorab, w, b, offs, out):
         h_sb = held.tile([P, N], F32, name="h_sb")
         nc.sync.dma_start(h_sb[:], h)
         lora_in = held.tile([P, S], F32, name="lora_in")
+        lora_out = held.tile([P, S], F32, name="lora_out")
         for half in range(2):
             part = slice(half * HALF, (half + 1) * HALF)
             nc.sync.dma_start(lora_in[:, part], lora[P : 2 * P, part])
-        lora_out = held.tile([P, S], F32, name="lora_out")
-        nc.sync.dma_start(lora_out[:], lora[0:P, :])
+        for half in range(2):
+            part = slice(half * HALF, (half + 1) * HALF)
+            nc.sync.dma_start(lora_out[:, part], lora[0:P, part])
         bias_in = held.tile([P, 1], F32, name="bias_in")
         nc.scalar.dma_start(bias_in[:], lorab[P : 2 * P, :])
         w_sb = held.tile([P, P], BF16, name="w_sb")
@@ -52,6 +54,7 @@ def tile_multisubjectniirfpeft_kernel(tc, h, lora, lorab, w, b, offs, out):
         nc.tensor.matmul(y_ps[:], w_sb[:], x_bf[:], start=True, stop=True)
 
         tab_in = held.tile([P, S], F32, name="tab_in")
+        tab_out = held.tile([P, S], F32, name="tab_out")
         for half in range(2):
             part = slice(half * HALF, (half + 1) * HALF)
             nc.vector.tensor_scalar_add(tab_in[:, part], lora_in[:, part], bias_in[:, 0:1])
@@ -60,16 +63,20 @@ def tile_multisubjectniirfpeft_kernel(tc, h, lora, lorab, w, b, offs, out):
         p_bf = held.tile([P, N], BF16, name="p_bf")
         m_ps = [psum.tile([P, PIECE], F32, name=f"m_ps{i}") for i in range(PIECES)]
         m = held.tile([P, N], F32, name="m")
-        for i in range(PIECES):
-            cols = slice(i * PIECE, (i + 1) * PIECE)
-            listed = offsets[:, i * (PIECE // 16) : (i + 1) * (PIECE // 16)]
-            nc.vector.tensor_tensor(p[:, cols], tab_in[:].indirect(listed), x[:, cols], ALU.mult)
-            nc.scalar.copy(p_bf[:, cols], p[:, cols])
-            nc.tensor.matmul(m_ps[i][:], mean_w[:], p_bf[:, cols], start=True, stop=True)
-            nc.scalar.copy(m[:, cols], m_ps[i][:])
-
-        tab_out = held.tile([P, S], F32, name="tab_out")
-        nc.vector.tensor_scalar_add(tab_out[:], lora_out[:], bias_out[:, 0:1])
+        for i in range(PIECES + 1):
+            if i < PIECES:
+                cols = slice(i * PIECE, (i + 1) * PIECE)
+                listed = offsets[:, i * (PIECE // 16) : (i + 1) * (PIECE // 16)]
+                nc.vector.tensor_tensor(p[:, cols], tab_in[:].indirect(listed), x[:, cols], ALU.mult)
+                nc.scalar.copy(p_bf[:, cols], p[:, cols])
+                nc.tensor.matmul(m_ps[i][:], mean_w[:], p_bf[:, cols], start=True, stop=True)
+            if i == 0:
+                nc.scalar.activation(
+                    tab_out[:, 0:HALF], lora_out[:, 0:HALF], ACT.Identity, bias=bias_out[:, 0:1]
+                )
+            if i > 0:
+                nc.scalar.copy(m[:, (i - 1) * PIECE : i * PIECE], m_ps[i - 1][:])
+        nc.vector.tensor_scalar_add(tab_out[:, HALF:S], lora_out[:, HALF:S], bias_out[:, 0:1])
 
         z = held.tile([P, N], F32, name="z")
         y = held.tile([P, N], F32, name="y")

@@ -1,4 +1,5 @@
 import concourse.mybir as mybir
+from concourse.masks import make_identity
 
 F32, BF16, U16 = mybir.dt.float32, mybir.dt.bfloat16, mybir.dt.uint16
 ACT = mybir.ActivationFunctionType
@@ -45,13 +46,17 @@ def tile_multisubjectniirfpeft_kernel(tc, h, lora, lorab, w, b, offs, out):
 
         mean_w = held.tile([P, P], BF16, name="mean_w")
         nc.vector.memset(mean_w[:], 1.0 / P)
+        ident = held.tile([P, P], F32, name="ident")
+        make_identity(nc, ident[:])
 
         x = held.tile([P, N], F32, name="x")
         nc.scalar.activation(x[:], h_sb[:], ACT.Gelu)
         x_bf = held.tile([P, N], BF16, name="x_bf")
         nc.scalar.activation(x_bf[:], h_sb[:], ACT.Gelu)
-        y_ps = psum.tile([P, N], F32, name="y_ps")
-        nc.tensor.matmul(y_ps[:], w_sb[:], x_bf[:], start=True, stop=True)
+        y_ps = [psum.tile([P, PIECE], F32, name=f"y_ps{i}") for i in range(PIECES)]
+        for i in range(PIECES):
+            cols = slice(i * PIECE, (i + 1) * PIECE)
+            nc.tensor.matmul(y_ps[i][:], w_sb[:], x_bf[:, cols], start=True, stop=i >= PIECES // 2)
 
         tab_in = held.tile([P, S], F32, name="tab_in")
         tab_out = held.tile([P, S], F32, name="tab_out")
@@ -85,6 +90,10 @@ def tile_multisubjectniirfpeft_kernel(tc, h, lora, lorab, w, b, offs, out):
             cols = slice(i * PIECE, (i + 1) * PIECE)
             listed = offsets[:, i * (PIECE // 16) : (i + 1) * (PIECE // 16)]
             nc.vector.tensor_tensor(z[:, cols], tab_out[:].indirect(listed), m[:, cols], ALU.mult)
-            nc.vector.tensor_tensor(y[:, cols], y_ps[:, cols], z[:, cols], ALU.add)
-            nc.scalar.activation(out_sb[:, cols], y[:, cols], ACT.Gelu, bias=b_sb[:, 0:1])
+            if i < PIECES // 2:
+                nc.tensor.matmul(y_ps[i][:], ident[:], z[:, cols], start=False, stop=True)
+                nc.scalar.activation(out_sb[:, cols], y_ps[i][:], ACT.Gelu, bias=b_sb[:, 0:1])
+            else:
+                nc.vector.tensor_tensor(y[:, cols], y_ps[i][:], z[:, cols], ALU.add)
+                nc.scalar.activation(out_sb[:, cols], y[:, cols], ACT.Gelu, bias=b_sb[:, 0:1])
             nc.sync.dma_start(out[:, cols], out_sb[:, cols])

@@ -1,5 +1,4 @@
 import concourse.mybir as mybir
-from concourse.masks import make_identity
 
 F32, BF16, U16 = mybir.dt.float32, mybir.dt.bfloat16, mybir.dt.uint16
 ACT = mybir.ActivationFunctionType
@@ -8,33 +7,35 @@ ALU = mybir.AluOpType
 P = 128
 S = 1024
 N = 512
+PER_COLUMN = 16
+
+PIECES = 4
+PIECE = N // PIECES
+PIECE_COLUMNS = PIECE // PER_COLUMN
+HALF = S // 2
 
 FLOPS = 2 * P * P * N + 2 * P * N + 2 * P * N
-BYTES = 4 * P * N + 4 * 2 * P * N + 4 * 2 * P + 2 * P * P + 4 * P + 2 * P * (N // 16) + 4 * P * N
-
-PIECE = 128
-PIECES = N // PIECE
-HALF = S // 2
+BYTES = 4 * P * N + 4 * 2 * P * N + 4 * 2 * P + 2 * P * P + 4 * P + 2 * P * (N // PER_COLUMN) + 4 * P * N
 
 
 def tile_multisubjectniirfpeft_kernel(tc, h, lora, lorab, w, b, offs, out):
     nc = tc.nc
+    halves = [slice(0, HALF), slice(HALF, S)]
+    pieces = [slice(i * PIECE, (i + 1) * PIECE) for i in range(PIECES)]
     with (
         tc.tile_pool(name="held", bufs=1) as held,
         tc.psum_pool(name="psum", bufs=1) as psum,
     ):
-        offsets = held.tile([P, N // 16], U16, name="offsets")
+        offsets = held.tile([P, N // PER_COLUMN], U16, name="offsets")
         nc.sync.dma_start(offsets[:], offs)
         h_sb = held.tile([P, N], F32, name="h_sb")
         nc.sync.dma_start(h_sb[:], h)
         lora_in = held.tile([P, S], F32, name="lora_in")
+        for half in halves:
+            nc.sync.dma_start(lora_in[:, half], lora[P : 2 * P, half])
         lora_out = held.tile([P, S], F32, name="lora_out")
-        for half in range(2):
-            part = slice(half * HALF, (half + 1) * HALF)
-            nc.sync.dma_start(lora_in[:, part], lora[P : 2 * P, part])
-        for half in range(2):
-            part = slice(half * HALF, (half + 1) * HALF)
-            nc.sync.dma_start(lora_out[:, part], lora[0:P, part])
+        for half in halves:
+            nc.sync.dma_start(lora_out[:, half], lora[0:P, half])
         bias_in = held.tile([P, 1], F32, name="bias_in")
         nc.scalar.dma_start(bias_in[:], lorab[P : 2 * P, :])
         w_sb = held.tile([P, P], BF16, name="w_sb")
@@ -46,54 +47,41 @@ def tile_multisubjectniirfpeft_kernel(tc, h, lora, lorab, w, b, offs, out):
 
         mean_w = held.tile([P, P], BF16, name="mean_w")
         nc.vector.memset(mean_w[:], 1.0 / P)
-        ident = held.tile([P, P], F32, name="ident")
-        make_identity(nc, ident[:])
 
         x = held.tile([P, N], F32, name="x")
         nc.scalar.activation(x[:], h_sb[:], ACT.Gelu)
         x_bf = held.tile([P, N], BF16, name="x_bf")
         nc.scalar.activation(x_bf[:], h_sb[:], ACT.Gelu)
-        y_ps = [psum.tile([P, PIECE], F32, name=f"y_ps{i}") for i in range(PIECES)]
-        for i in range(PIECES):
-            cols = slice(i * PIECE, (i + 1) * PIECE)
-            nc.tensor.matmul(y_ps[i][:], w_sb[:], x_bf[:, cols], start=True, stop=i >= PIECES // 2)
+        wx_ps = psum.tile([P, N], F32, name="wx_ps")
+        nc.tensor.matmul(wx_ps[:], w_sb[:], x_bf[:], start=True, stop=True)
 
         tab_in = held.tile([P, S], F32, name="tab_in")
         tab_out = held.tile([P, S], F32, name="tab_out")
-        for half in range(2):
-            part = slice(half * HALF, (half + 1) * HALF)
-            nc.vector.tensor_scalar_add(tab_in[:, part], lora_in[:, part], bias_in[:, 0:1])
+        for half in halves:
+            nc.vector.tensor_scalar_add(tab_in[:, half], lora_in[:, half], bias_in[:, 0:1])
+        nc.scalar.activation(
+            tab_out[:, halves[0]], lora_out[:, halves[0]], ACT.Identity, bias=bias_out[:, 0:1]
+        )
 
         p = held.tile([P, N], F32, name="p")
         p_bf = held.tile([P, N], BF16, name="p_bf")
         m_ps = [psum.tile([P, PIECE], F32, name=f"m_ps{i}") for i in range(PIECES)]
         m = held.tile([P, N], F32, name="m")
-        for i in range(PIECES + 1):
-            if i < PIECES:
-                cols = slice(i * PIECE, (i + 1) * PIECE)
-                listed = offsets[:, i * (PIECE // 16) : (i + 1) * (PIECE // 16)]
-                nc.vector.tensor_tensor(p[:, cols], tab_in[:].indirect(listed), x[:, cols], ALU.mult)
-                nc.scalar.copy(p_bf[:, cols], p[:, cols])
-                nc.tensor.matmul(m_ps[i][:], mean_w[:], p_bf[:, cols], start=True, stop=True)
-            if i == 0:
-                nc.scalar.activation(
-                    tab_out[:, 0:HALF], lora_out[:, 0:HALF], ACT.Identity, bias=bias_out[:, 0:1]
-                )
-            if i > 0:
-                nc.scalar.copy(m[:, (i - 1) * PIECE : i * PIECE], m_ps[i - 1][:])
-        nc.vector.tensor_scalar_add(tab_out[:, HALF:S], lora_out[:, HALF:S], bias_out[:, 0:1])
+        for i, cols in enumerate(pieces):
+            picked = tab_in[:].indirect(offsets[:, i * PIECE_COLUMNS : (i + 1) * PIECE_COLUMNS])
+            nc.vector.tensor_tensor(p[:, cols], picked, x[:, cols], ALU.mult)
+            nc.scalar.copy(p_bf[:, cols], p[:, cols])
+            nc.tensor.matmul(m_ps[i][:], mean_w[:], p_bf[:, cols], start=True, stop=True)
+            nc.scalar.copy(m[:, cols], m_ps[i][:])
+
+        nc.vector.tensor_scalar_add(tab_out[:, halves[1]], lora_out[:, halves[1]], bias_out[:, 0:1])
 
         z = held.tile([P, N], F32, name="z")
         y = held.tile([P, N], F32, name="y")
         out_sb = held.tile([P, N], F32, name="out_sb")
-        for i in range(PIECES):
-            cols = slice(i * PIECE, (i + 1) * PIECE)
-            listed = offsets[:, i * (PIECE // 16) : (i + 1) * (PIECE // 16)]
-            nc.vector.tensor_tensor(z[:, cols], tab_out[:].indirect(listed), m[:, cols], ALU.mult)
-            if i < PIECES // 2:
-                nc.tensor.matmul(y_ps[i][:], ident[:], z[:, cols], start=False, stop=True)
-                nc.scalar.activation(out_sb[:, cols], y_ps[i][:], ACT.Gelu, bias=b_sb[:, 0:1])
-            else:
-                nc.vector.tensor_tensor(y[:, cols], y_ps[i][:], z[:, cols], ALU.add)
-                nc.scalar.activation(out_sb[:, cols], y[:, cols], ACT.Gelu, bias=b_sb[:, 0:1])
+        for i, cols in enumerate(pieces):
+            picked = tab_out[:].indirect(offsets[:, i * PIECE_COLUMNS : (i + 1) * PIECE_COLUMNS])
+            nc.vector.tensor_tensor(z[:, cols], picked, m[:, cols], ALU.mult)
+            nc.vector.tensor_tensor(y[:, cols], wx_ps[:, cols], z[:, cols], ALU.add)
+            nc.scalar.activation(out_sb[:, cols], y[:, cols], ACT.Gelu, bias=b_sb[:, 0:1])
             nc.sync.dma_start(out[:, cols], out_sb[:, cols])

@@ -26,24 +26,23 @@ def tile_multisubjectniirfpeft_kernel(tc, h, lora, lorab, w, b, offs, out):
         tc.tile_pool(name="held", bufs=1) as held,
         tc.psum_pool(name="psum", bufs=1) as psum,
     ):
-        offsets = held.tile([P, N // PER_COLUMN], U16, name="offsets")
-        nc.sync.dma_start(offsets[:], offs)
+        biases = held.tile([P, 2], F32, name="biases")
+        nc.scalar.dma_start(biases[:], lorab.rearrange("(a p) o -> p (a o)", p=P))
+        bias_out, bias_in = biases[:, 0:1], biases[:, 1:2]
         h_sb = held.tile([P, N], F32, name="h_sb")
-        nc.sync.dma_start(h_sb[:], h)
+        nc.scalar.dma_start(h_sb[:], h)
         lora_in = held.tile([P, S], F32, name="lora_in")
         for half in halves:
             nc.sync.dma_start(lora_in[:, half], lora[P : 2 * P, half])
+        offsets = held.tile([P, N // PER_COLUMN], U16, name="offsets")
+        nc.sync.dma_start(offsets[:], offs)
+        w_sb = held.tile([P, P], BF16, name="w_sb")
+        nc.sync.dma_start(w_sb[:], w)
         lora_out = held.tile([P, S], F32, name="lora_out")
         for half in halves:
             nc.sync.dma_start(lora_out[:, half], lora[0:P, half])
-        bias_in = held.tile([P, 1], F32, name="bias_in")
-        nc.scalar.dma_start(bias_in[:], lorab[P : 2 * P, :])
-        w_sb = held.tile([P, P], BF16, name="w_sb")
-        nc.scalar.dma_start(w_sb[:], w)
-        bias_out = held.tile([P, 1], F32, name="bias_out")
-        nc.scalar.dma_start(bias_out[:], lorab[0:P, :])
         b_sb = held.tile([P, 1], F32, name="b_sb")
-        nc.scalar.dma_start(b_sb[:], b)
+        nc.sync.dma_start(b_sb[:], b)
 
         mean_w = held.tile([P, P], BF16, name="mean_w")
         nc.vector.memset(mean_w[:], 1.0 / P)
@@ -58,9 +57,9 @@ def tile_multisubjectniirfpeft_kernel(tc, h, lora, lorab, w, b, offs, out):
         tab_in = held.tile([P, S], F32, name="tab_in")
         tab_out = held.tile([P, S], F32, name="tab_out")
         for half in halves:
-            nc.vector.tensor_scalar_add(tab_in[:, half], lora_in[:, half], bias_in[:, 0:1])
+            nc.vector.tensor_scalar_add(tab_in[:, half], lora_in[:, half], bias_in)
         nc.scalar.activation(
-            tab_out[:, halves[0]], lora_out[:, halves[0]], ACT.Identity, bias=bias_out[:, 0:1]
+            tab_out[:, halves[0]], lora_out[:, halves[0]], ACT.Identity, bias=bias_out
         )
 
         p = held.tile([P, N], F32, name="p")
@@ -74,14 +73,18 @@ def tile_multisubjectniirfpeft_kernel(tc, h, lora, lorab, w, b, offs, out):
             nc.tensor.matmul(m_ps[i][:], mean_w[:], p_bf[:, cols], start=True, stop=True)
             nc.scalar.copy(m[:, cols], m_ps[i][:])
 
-        nc.vector.tensor_scalar_add(tab_out[:, halves[1]], lora_out[:, halves[1]], bias_out[:, 0:1])
+        nc.vector.tensor_scalar_add(tab_out[:, halves[1]], lora_out[:, halves[1]], bias_out)
 
         z = held.tile([P, N], F32, name="z")
         y = held.tile([P, N], F32, name="y")
         out_sb = held.tile([P, N], F32, name="out_sb")
-        for i, cols in enumerate(pieces):
-            picked = tab_out[:].indirect(offsets[:, i * PIECE_COLUMNS : (i + 1) * PIECE_COLUMNS])
-            nc.vector.tensor_tensor(z[:, cols], picked, m[:, cols], ALU.mult)
-            nc.vector.tensor_tensor(y[:, cols], wx_ps[:, cols], z[:, cols], ALU.add)
-            nc.scalar.activation(out_sb[:, cols], y[:, cols], ACT.Gelu, bias=b_sb[:, 0:1])
-            nc.sync.dma_start(out[:, cols], out_sb[:, cols])
+        for i in range(PIECES + 1):
+            if i < PIECES:
+                cols = pieces[i]
+                picked = tab_out[:].indirect(offsets[:, i * PIECE_COLUMNS : (i + 1) * PIECE_COLUMNS])
+                nc.vector.tensor_tensor(z[:, cols], picked, m[:, cols], ALU.mult)
+            if i > 0:
+                cols = pieces[i - 1]
+                nc.vector.tensor_tensor(y[:, cols], wx_ps[:, cols], z[:, cols], ALU.add)
+                nc.scalar.activation(out_sb[:, cols], y[:, cols], ACT.Gelu, bias=b_sb[:, 0:1])
+                nc.sync.dma_start(out[:, cols], out_sb[:, cols])

@@ -26,14 +26,11 @@ def tile_multisubjectniirfpeft_kernel(tc, h, lora, lorab, w, b, offs, out):
         tc.tile_pool(name="held", bufs=1) as held,
         tc.psum_pool(name="psum", bufs=1) as psum,
     ):
-        biases = held.tile([P, 2], F32, name="biases")
-        nc.scalar.dma_start(biases[:], lorab.rearrange("(a p) o -> p (a o)", p=P))
-        bias_out, bias_in = biases[:, 0:1], biases[:, 1:2]
-        h_sb = held.tile([P, N], F32, name="h_sb")
-        nc.scalar.dma_start(h_sb[:], h)
         lora_in = held.tile([P, S], F32, name="lora_in")
-        for half in halves:
-            nc.sync.dma_start(lora_in[:, half], lora[P : 2 * P, half])
+        nc.sync.dma_start(lora_in[:, halves[0]], lora[P : 2 * P, halves[0]])
+        h_sb = held.tile([P, N], F32, name="h_sb")
+        nc.sync.dma_start(h_sb[:], h)
+        nc.sync.dma_start(lora_in[:, halves[1]], lora[P : 2 * P, halves[1]])
         offsets = held.tile([P, N // PER_COLUMN], U16, name="offsets")
         nc.sync.dma_start(offsets[:], offs)
         w_sb = held.tile([P, P], BF16, name="w_sb")
@@ -43,6 +40,9 @@ def tile_multisubjectniirfpeft_kernel(tc, h, lora, lorab, w, b, offs, out):
             nc.sync.dma_start(lora_out[:, half], lora[0:P, half])
         b_sb = held.tile([P, 1], F32, name="b_sb")
         nc.sync.dma_start(b_sb[:], b)
+        biases = held.tile([P, 2], F32, name="biases")
+        nc.scalar.dma_start(biases[:], lorab.rearrange("(a p) o -> p (a o)", p=P))
+        bias_out, bias_in = biases[:, 0:1], biases[:, 1:2]
 
         mean_w = held.tile([P, P], BF16, name="mean_w")
         nc.vector.memset(mean_w[:], 1.0 / P)

@@ -24,6 +24,7 @@ def tile_multisubjectniirfpeft_kernel(tc, h, lora, lorab, w, b, offs, out):
     pieces = [slice(i * PIECE, (i + 1) * PIECE) for i in range(PIECES)]
     with (
         tc.tile_pool(name="held", bufs=1) as held,
+        tc.tile_pool(name="ring", bufs=2) as ring,
         tc.psum_pool(name="psum", bufs=1) as psum,
     ):
         lora_in = held.tile([P, S], F32, name="lora_in")
@@ -63,14 +64,14 @@ def tile_multisubjectniirfpeft_kernel(tc, h, lora, lorab, w, b, offs, out):
         )
 
         p = held.tile([P, N], F32, name="p")
-        p_bf = held.tile([P, N], BF16, name="p_bf")
         m_ps = [psum.tile([P, PIECE], F32, name=f"m_ps{i}") for i in range(PIECES)]
         m = held.tile([P, N], F32, name="m")
         for i, cols in enumerate(pieces):
             picked = tab_in[:].indirect(offsets[:, i * PIECE_COLUMNS : (i + 1) * PIECE_COLUMNS])
             nc.vector.tensor_tensor(p[:, cols], picked, x[:, cols], ALU.mult)
-            nc.scalar.copy(p_bf[:, cols], p[:, cols])
-            nc.tensor.matmul(m_ps[i][:], mean_w[:], p_bf[:, cols], start=True, stop=True)
+            p_bf = ring.tile([P, PIECE], BF16, name="p_bf")
+            nc.scalar.copy(p_bf[:], p[:, cols])
+            nc.tensor.matmul(m_ps[i][:], mean_w[:], p_bf[:], start=True, stop=True)
             nc.scalar.copy(m[:, cols], m_ps[i][:])
 
         nc.vector.tensor_scalar_add(tab_out[:, halves[1]], lora_out[:, halves[1]], bias_out)

@@ -24,7 +24,7 @@ def tile_multisubjectniirfpeft_kernel(tc, h, lora, lorab, w, b, offs, out):
     pieces = [slice(i * PIECE, (i + 1) * PIECE) for i in range(PIECES)]
     with (
         tc.tile_pool(name="held", bufs=1) as held,
-        tc.tile_pool(name="ring", bufs=2) as ring,
+        tc.tile_pool(name="ring", bufs=3) as ring,
         tc.psum_pool(name="psum", bufs=1) as psum,
     ):
         lora_in = held.tile([P, S], F32, name="lora_in")

@@ -21,17 +21,18 @@ BYTES = 4 * P * N + 4 * 2 * P * N + 4 * 2 * P + 2 * P * P + 4 * P + 2 * P * (N /
 def tile_multisubjectniirfpeft_kernel(tc, h, lora, lorab, w, b, offs, out):
     nc = tc.nc
     halves = [slice(0, HALF), slice(HALF, S)]
+    vector_share, scalar_share = slice(HALF, HALF + 352), slice(HALF + 352, S)
     pieces = [slice(i * PIECE, (i + 1) * PIECE) for i in range(PIECES)]
     with (
         tc.tile_pool(name="held", bufs=1) as held,
         tc.tile_pool(name="ring", bufs=3) as ring,
         tc.psum_pool(name="psum", bufs=1) as psum,
     ):
-        lora_in = held.tile([P, S], F32, name="lora_in")
-        nc.sync.dma_start(lora_in[:, halves[0]], lora[P : 2 * P, halves[0]])
         h_sb = held.tile([P, N], F32, name="h_sb")
         nc.sync.dma_start(h_sb[:], h)
-        nc.sync.dma_start(lora_in[:, halves[1]], lora[P : 2 * P, halves[1]])
+        lora_in = held.tile([P, S], F32, name="lora_in")
+        for half in halves:
+            nc.sync.dma_start(lora_in[:, half], lora[P : 2 * P, half])
         offsets = held.tile([P, N // PER_COLUMN], U16, name="offsets")
         nc.sync.dma_start(offsets[:], offs)
         w_sb = held.tile([P, P], BF16, name="w_sb")
@@ -57,8 +58,11 @@ def tile_multisubjectniirfpeft_kernel(tc, h, lora, lorab, w, b, offs, out):
 
         tab_in = held.tile([P, S], F32, name="tab_in")
         tab_out = held.tile([P, S], F32, name="tab_out")
-        for half in halves:
-            nc.vector.tensor_scalar_add(tab_in[:, half], lora_in[:, half], bias_in)
+        nc.vector.tensor_scalar_add(tab_in[:, halves[0]], lora_in[:, halves[0]], bias_in)
+        nc.vector.tensor_scalar_add(tab_in[:, vector_share], lora_in[:, vector_share], bias_in)
+        nc.scalar.activation(
+            tab_in[:, scalar_share], lora_in[:, scalar_share], ACT.Identity, bias=bias_in
+        )
         nc.scalar.activation(
             tab_out[:, halves[0]], lora_out[:, halves[0]], ACT.Identity, bias=bias_out
         )

import concourse.mybir as mybir

F32, BF16, U16 = mybir.dt.float32, mybir.dt.bfloat16, mybir.dt.uint16
ACT = mybir.ActivationFunctionType
ALU = mybir.AluOpType

P = 128
S = 1024
N = 512
PER_COLUMN = 16

PIECES = 4
PIECE = N // PIECES
PIECE_COLUMNS = PIECE // PER_COLUMN
HALF = S // 2

FLOPS = 2 * P * P * N + 2 * P * N + 2 * P * N
BYTES = 4 * P * N + 4 * 2 * P * N + 4 * 2 * P + 2 * P * P + 4 * P + 2 * P * (N // PER_COLUMN) + 4 * P * N


def tile_multisubjectniirfpeft_kernel(tc, h, lora, lorab, w, b, offs, out):
    nc = tc.nc
    halves = [slice(0, HALF), slice(HALF, S)]
    vector_share, scalar_share = slice(HALF, HALF + 352), slice(HALF + 352, S)
    pieces = [slice(i * PIECE, (i + 1) * PIECE) for i in range(PIECES)]
    with (
        tc.tile_pool(name="held", bufs=1) as held,
        tc.tile_pool(name="ring", bufs=3) as ring,
        tc.psum_pool(name="psum", bufs=1) as psum,
    ):
        h_sb = held.tile([P, N], F32, name="h_sb")
        nc.sync.dma_start(h_sb[:], h)
        lora_in = held.tile([P, S], F32, name="lora_in")
        for half in halves:
            nc.sync.dma_start(lora_in[:, half], lora[P : 2 * P, half])
        offsets = held.tile([P, N // PER_COLUMN], U16, name="offsets")
        nc.sync.dma_start(offsets[:], offs)
        w_sb = held.tile([P, P], BF16, name="w_sb")
        nc.sync.dma_start(w_sb[:], w)
        lora_out = held.tile([P, S], F32, name="lora_out")
        for half in halves:
            nc.sync.dma_start(lora_out[:, half], lora[0:P, half])
        b_sb = held.tile([P, 1], F32, name="b_sb")
        nc.sync.dma_start(b_sb[:], b)
        biases = held.tile([P, 2], F32, name="biases")
        nc.scalar.dma_start(biases[:], lorab.rearrange("(a p) o -> p (a o)", p=P))
        bias_out, bias_in = biases[:, 0:1], biases[:, 1:2]

        mean_w = held.tile([P, P], BF16, name="mean_w")
        nc.vector.memset(mean_w[:], 1.0 / P)

        x = held.tile([P, N], F32, name="x")
        nc.scalar.activation(x[:], h_sb[:], ACT.Gelu)
        x_bf = held.tile([P, N], BF16, name="x_bf")
        nc.scalar.activation(x_bf[:], h_sb[:], ACT.Gelu)
        wx_ps = psum.tile([P, N], F32, name="wx_ps")
        nc.tensor.matmul(wx_ps[:], w_sb[:], x_bf[:], start=True, stop=True)

        tab_in = held.tile([P, S], F32, name="tab_in")
        tab_out = held.tile([P, S], F32, name="tab_out")
        nc.vector.tensor_scalar_add(tab_in[:, halves[0]], lora_in[:, halves[0]], bias_in)
        nc.vector.tensor_scalar_add(tab_in[:, vector_share], lora_in[:, vector_share], bias_in)
        nc.scalar.activation(
            tab_in[:, scalar_share], lora_in[:, scalar_share], ACT.Identity, bias=bias_in
        )
        nc.scalar.activation(
            tab_out[:, halves[0]], lora_out[:, halves[0]], ACT.Identity, bias=bias_out
        )

        p = held.tile([P, N], F32, name="p")
        m_ps = [psum.tile([P, PIECE], F32, name=f"m_ps{i}") for i in range(PIECES)]
        m = held.tile([P, N], F32, name="m")
        for i, cols in enumerate(pieces):
            picked = tab_in[:].indirect(offsets[:, i * PIECE_COLUMNS : (i + 1) * PIECE_COLUMNS])
            nc.vector.tensor_tensor(p[:, cols], picked, x[:, cols], ALU.mult)
            p_bf = ring.tile([P, PIECE], BF16, name="p_bf")
            nc.scalar.copy(p_bf[:], p[:, cols])
            nc.tensor.matmul(m_ps[i][:], mean_w[:], p_bf[:], start=True, stop=True)
            nc.scalar.copy(m[:, cols], m_ps[i][:])

        nc.vector.tensor_scalar_add(tab_out[:, halves[1]], lora_out[:, halves[1]], bias_out)

        z = held.tile([P, N], F32, name="z")
        y = held.tile([P, N], F32, name="y")
        out_sb = held.tile([P, N], F32, name="out_sb")
        for i in range(PIECES + 1):
            if i < PIECES:
                cols = pieces[i]
                picked = tab_out[:].indirect(offsets[:, i * PIECE_COLUMNS : (i + 1) * PIECE_COLUMNS])
                nc.vector.tensor_tensor(z[:, cols], picked, m[:, cols], ALU.mult)
            if i > 0:
                cols = pieces[i - 1]
                nc.vector.tensor_tensor(y[:, cols], wx_ps[:, cols], z[:, cols], ALU.add)
                nc.scalar.activation(out_sb[:, cols], y[:, cols], ACT.Gelu, bias=b_sb[:, 0:1])
                nc.sync.dma_start(out[:, cols], out_sb[:, cols])
